import numpy as np
import ml_dtypes


def mxq(x, axis, fmt="e4m3"):
    dtype, down = {"e4m3": (ml_dtypes.float8_e4m3fn, 7), "e5m2": (ml_dtypes.float8_e5m2, 14)}[fmt]
    v = np.moveaxis(np.asarray(x, np.float32).astype(ml_dtypes.bfloat16).astype(np.float64), axis, -1)
    blocks = v.reshape(v.shape[:-1] + (-1, 32))
    amax = np.abs(blocks).max(-1, keepdims=True)
    byte = np.maximum(np.where(amax > 0, np.frexp(amax)[1] - 1 + 127, 0) - down, 1)
    scale = np.exp2(byte - 127.0)
    codes = (blocks / scale).astype(np.float32).astype(dtype).astype(np.float64)
    return np.moveaxis((codes * scale).reshape(v.shape), -1, axis)


WIDE = False


def mx_kscale(k):
    if not WIDE:
        return np.ones(k)
    levels = np.array([10, -10, 5, -5, 0])
    a = np.random.permutation(np.resize(levels, k // 512 * 4)).reshape(k // 512, 4)
    idx = np.arange(k)
    return np.exp2(a[idx // 512, idx % 128 // 32])


BF16 = ml_dtypes.bfloat16


def bf(x):
    return np.asarray(x, np.float32).astype(BF16)


def f64(x):
    return np.asarray(x).astype(np.float64)


N_A, N_P, D = 2048, 2048, 512
TEMPERATURE = 0.07
SIG = 3.5
SA = np.sqrt(SIG * TEMPERATURE / np.sqrt(D))
SP = SA * np.sqrt(SIG ** 2 - 2.0 * np.log(N_P / N_A)) / SIG


def logsumexp(v):
    m = v.max(axis=1, keepdims=True)
    return m[:, 0] + np.log(np.exp(v - m).sum(axis=1))


def setup_inputs():
    s = mx_kscale(D)
    c = np.mean(s ** 4) ** -0.25
    return {"anchor": bf(np.random.standard_normal((N_A, D)) * SA * s * c),
            "pos": bf(np.random.standard_normal((N_P, D)) * SP / (s * c))}


def reference(anchor, pos):
    aq = mxq(f64(anchor), 1, "e4m3")
    sim_pos = (aq @ mxq(f64(pos), 1, "e4m3").T) / TEMPERATURE
    sim_neg = (aq @ aq.T) / TEMPERATURE
    sim_neg = np.where(np.eye(aq.shape[0], dtype=bool), -np.inf, sim_neg)
    numerator = logsumexp(sim_pos)
    denominator = np.logaddexp(numerator, logsumexp(sim_neg))
    return numerator - denominator

@@ -1,0 +1,207 @@
+from contextlib import ExitStack
+
+import concourse.mybir as mybir
+from concourse.masks import make_identity
+
+F32 = mybir.dt.float32
+BF16 = mybir.dt.bfloat16
+U32 = mybir.dt.uint32
+U8 = mybir.dt.uint8
+FP8X4 = mybir.dt.float8_e4m3fn_x4
+ALU = mybir.AluOpType
+ACT = mybir.ActivationFunctionType
+AXIS_X = mybir.AxisListType.X
+
+P = 128
+PACK = 4
+ROWS = 2048
+FEATURES = 512
+ROW_TILES = ROWS // P
+BANK = 512
+CHUNK_TILES = BANK // P
+CHUNKS = ROW_TILES // CHUNK_TILES
+HALVES = 2
+POS, NEG = 0, 1
+PARTS = 2 * CHUNKS
+TEMPERATURE = 0.07
+MASK_ROOT = 2.0**50
+
+FLOPS = 2 * 2 * ROWS * ROWS * FEATURES
+
+
+def tile_crossgenderinfonceloss_pa_kernel(tc, anchor, pos, out):
+    nc = tc.nc
+    with ExitStack() as stack:
+        keep = stack.enter_context(tc.tile_pool(name="keep", bufs=1))
+        stage = stack.enter_context(tc.tile_pool(name="stage", bufs=3))
+        unread = stack.enter_context(tc.tile_pool(name="unread", bufs=4))
+        psum = stack.enter_context(tc.psum_pool(name="psum", bufs=8))
+
+        raw = {}
+        for name in ("anchor", "pos"):
+            raw[name] = keep.tile([P, ROW_TILES, FEATURES], BF16, name="raw_" + name)
+        for chunk in range(CHUNKS):
+            tiles = slice(chunk * CHUNK_TILES, (chunk + 1) * CHUNK_TILES)
+            for name, source in (("anchor", anchor), ("pos", pos)):
+                nc.sync.dma_start(
+                    out=raw[name][:, tiles, :],
+                    in_=source.rearrange("(p r) k -> p r k", r=ROW_TILES)[:, tiles, :],
+                )
+
+        identity = keep.tile([P, P], F32)
+        make_identity(nc, identity[:])
+        zero = keep.tile([P, 1], F32)
+        nc.vector.memset(zero[:], 0.0)
+        one = keep.tile([P, 1], F32)
+        nc.scalar.activation(out=one[:], in_=zero[:], func=ACT.Exp)
+
+        mask_values = keep.tile([P, 2, P, PACK], BF16, align_bytes=64)
+        spread_identity = identity[:].unsqueeze(2).to_broadcast([P, P, PACK])
+        nc.vector.tensor_scalar(
+            out=mask_values[:, 0], in0=spread_identity, scalar1=MASK_ROOT, scalar2=None, op0=ALU.mult
+        )
+        nc.vector.tensor_scalar(
+            out=mask_values[:, 1], in0=spread_identity, scalar1=-MASK_ROOT, scalar2=None, op0=ALU.mult
+        )
+        mask_codes = keep.tile([P, 2 * P], U32, align_bytes=64)
+        mask_scales = keep.tile([P, 2 * P], U8, align_bytes=64)
+        nc.vector.quantize_mx(
+            out=mask_codes[:].bitcast(FP8X4),
+            scales=mask_scales[:],
+            in_=mask_values[:].rearrange("p s m j -> p (s m j)"),
+        )
+
+        codes = {}
+        scales = {}
+        for name in ("anchor", "pos"):
+            codes[name] = keep.tile([P, ROWS], U32, name="codes_" + name, align_bytes=64)
+            scales[name] = keep.tile([P, ROWS], U8, name="scales_" + name, align_bytes=64)
+
+        top = keep.tile([P, ROW_TILES * PARTS], F32)
+        shift = keep.tile([P, ROW_TILES * PARTS], F32)
+        total = keep.tile([P, ROW_TILES * PARTS], F32)
+
+        def quantise_chunk(name, chunk):
+            words = raw[name][:].bitcast(F32)
+            grouped = stage.tile([P, BANK, PACK], BF16, align_bytes=64)
+            grouped_words = grouped[:].bitcast(F32)
+            for pair in range(2):
+                flipped = psum.tile([P, 2, HALVES, P], F32, tag="bank")
+                for t in range(2):
+                    r = chunk * CHUNK_TILES + 2 * pair + t
+                    for u in range(HALVES):
+                        nc.tensor.transpose(
+                            flipped[:, t, u, :], words[:, r, u * P : (u + 1) * P], identity[:]
+                        )
+                target = grouped_words[:, 2 * pair * P : 2 * (pair + 1) * P, :]
+                target = target.rearrange("p (t r) u -> p t r u", t=2)
+                source = flipped[:].rearrange("p t u r -> p t r u")
+                if pair == 0:
+                    nc.vector.tensor_copy(out=target, in_=source)
+                else:
+                    nc.scalar.copy(out=target, in_=source)
+            cols = slice(chunk * BANK, (chunk + 1) * BANK)
+            nc.vector.quantize_mx(
+                out=codes[name][:, cols].bitcast(FP8X4),
+                scales=scales[name][:, cols],
+                in_=grouped[:].rearrange("p w j -> p (w j)"),
+            )
+
+        def product(acc, r, name, cols, start, stop):
+            rows = slice(r * P, (r + 1) * P)
+            nc.tensor.matmul_mx(
+                out=acc,
+                lhsT=codes["anchor"][:, rows].bitcast(FP8X4),
+                lhsT_scale=scales["anchor"][:, rows],
+                rhs=codes[name][:, cols].bitcast(FP8X4),
+                rhs_scale=scales[name][:, cols],
+                start=start,
+                stop=stop,
+            )
+
+        def bank_of_logits(r, x, chunk):
+            acc = psum.tile([P, BANK], F32, tag="bank")
+            if x == NEG and chunk == r // CHUNK_TILES:
+                for t in range(CHUNK_TILES):
+                    other = chunk * CHUNK_TILES + t
+                    part = acc[:, t * P : (t + 1) * P]
+                    product(part, r, "anchor", slice(other * P, (other + 1) * P), True, other != r)
+                    if other == r:
+                        nc.tensor.matmul_mx(
+                            out=part,
+                            lhsT=mask_codes[:, 0:P].bitcast(FP8X4),
+                            lhsT_scale=mask_scales[:, 0:P],
+                            rhs=mask_codes[:, P : 2 * P].bitcast(FP8X4),
+                            rhs_scale=mask_scales[:, P : 2 * P],
+                            start=False,
+                            stop=True,
+                        )
+            else:
+                name = "pos" if x == POS else "anchor"
+                product(acc[:], r, name, slice(chunk * BANK, (chunk + 1) * BANK), True, True)
+            col = slice(r * PARTS + x * CHUNKS + chunk, r * PARTS + x * CHUNKS + chunk + 1)
+            nc.vector.tensor_reduce(out=top[:, col], in_=acc[:], axis=AXIS_X, op=ALU.max)
+            nc.gpsimd.tensor_scalar(
+                out=shift[:, col],
+                in0=top[:, col],
+                scalar1=-1.0 / TEMPERATURE,
+                scalar2=0.0,
+                op0=ALU.mult,
+                op1=ALU.add,
+            )
+            exps = unread.tile([P, BANK], BF16)
+            nc.scalar.activation(
+                out=exps[:],
+                in_=acc[:],
+                func=ACT.Exp,
+                bias=shift[:, col],
+                scale=1.0 / TEMPERATURE,
+                accum_out=total[:, col],
+            )
+
+        for s in range(CHUNKS):
+            quantise_chunk("anchor", s)
+            quantise_chunk("pos", s)
+            for r in range((s + 1) * CHUNK_TILES):
+                for chunk in range(s + 1):
+                    if r // CHUNK_TILES == s or chunk == s:
+                        bank_of_logits(r, NEG, chunk)
+                        bank_of_logits(r, POS, chunk)
+
+        shift_r = shift[:].rearrange("p (r b) -> p r b", b=PARTS)
+        total_r = total[:].rearrange("p (r b) -> p r b", b=PARTS)
+        low_all = keep.tile([P, ROW_TILES], F32)
+        low_pos = keep.tile([P, ROW_TILES], F32)
+        nc.vector.tensor_reduce(out=low_all[:], in_=shift_r, axis=AXIS_X, op=ALU.min)
+        nc.vector.tensor_reduce(out=low_pos[:], in_=shift_r[:, :, 0:CHUNKS], axis=AXIS_X, op=ALU.min)
+        weight = keep.tile([P, ROW_TILES, PARTS + CHUNKS], F32)
+        nc.vector.tensor_tensor(
+            out=weight[:, :, 0:PARTS],
+            in0=low_all[:].unsqueeze(2).to_broadcast([P, ROW_TILES, PARTS]),
+            in1=shift_r,
+            op=ALU.subtract,
+        )
+        nc.vector.tensor_tensor(
+            out=weight[:, :, PARTS:],
+            in0=low_pos[:].unsqueeze(2).to_broadcast([P, ROW_TILES, CHUNKS]),
+            in1=shift_r[:, :, 0:CHUNKS],
+            op=ALU.subtract,
+        )
+        nc.scalar.activation(out=weight[:], in_=weight[:], func=ACT.Exp)
+        nc.vector.tensor_tensor(
+            out=weight[:, :, 0:PARTS], in0=weight[:, :, 0:PARTS], in1=total_r, op=ALU.mult
+        )
+        nc.vector.tensor_tensor(
+            out=weight[:, :, PARTS:], in0=weight[:, :, PARTS:], in1=total_r[:, :, 0:CHUNKS], op=ALU.mult
+        )
+        sums = keep.tile([P, 2, ROW_TILES], F32)
+        nc.vector.tensor_reduce(out=sums[:, 0, :], in_=weight[:, :, PARTS:], axis=AXIS_X, op=ALU.add)
+        nc.vector.tensor_reduce(out=sums[:, 1, :], in_=weight[:, :, 0:PARTS], axis=AXIS_X, op=ALU.add)
+        logs = keep.tile([P, 2, ROW_TILES], F32)
+        nc.scalar.activation(out=logs[:], in_=sums[:], func=ACT.Ln)
+        gap = keep.tile([P, ROW_TILES], F32)
+        nc.vector.tensor_tensor(out=gap[:], in0=low_all[:], in1=low_pos[:], op=ALU.subtract)
+        result = keep.tile([P, ROW_TILES], F32)
+        nc.vector.tensor_tensor(out=result[:], in0=logs[:, 0, :], in1=logs[:, 1, :], op=ALU.subtract)
+        nc.vector.tensor_tensor(out=result[:], in0=result[:], in1=gap[:], op=ALU.add)
+        nc.sync.dma_start(out=out.rearrange("(p r) -> p r", r=ROW_TILES), in_=result[:])

@@ -18,34 +18,58 @@ ROWS = 2048
 FEATURES = 512
 ROW_TILES = ROWS // P
 BANK = 512
+PSUM_BANKS = 8
 CHUNK_TILES = BANK // P
 CHUNKS = ROW_TILES // CHUNK_TILES
-HALVES = 2
+HALF_TILES = CHUNK_TILES // 2
+WORD_HALVES = 2
 POS, NEG = 0, 1
 PARTS = 2 * CHUNKS
 TEMPERATURE = 0.07
 MASK_ROOT = 2.0**50
+FAR_BELOW = -1.0e30
+
+CHUNK_ORDER = [("anchor", c) for c in range(CHUNKS)] + [("pos", c) for c in range(CHUNKS)]
+STEPS_PER_CHUNK = 3
+HEAD_STEPS = 2 * STEPS_PER_CHUNK + 2
+LEAD = 2
 
 FLOPS = 2 * 2 * ROWS * ROWS * FEATURES
+
+
+def banks_opened_by(stage):
+    name, chunk = CHUNK_ORDER[stage]
+    if name == "pos":
+        return [(r, POS, chunk) for r in range(ROW_TILES)]
+    return [
+        (r, NEG, c)
+        for r in range((chunk + 1) * CHUNK_TILES)
+        for c in range(chunk + 1)
+        if r // CHUNK_TILES == chunk or c == chunk
+    ]
 
 
 def tile_crossgenderinfonceloss_pa_kernel(tc, anchor, pos, out):
     nc = tc.nc
     with ExitStack() as stack:
+        stack.enter_context(tc.manual_schedule())
         keep = stack.enter_context(tc.tile_pool(name="keep", bufs=1))
-        stage = stack.enter_context(tc.tile_pool(name="stage", bufs=3))
+        stage_pool = stack.enter_context(tc.tile_pool(name="stage", bufs=3))
         unread = stack.enter_context(tc.tile_pool(name="unread", bufs=4))
-        psum = stack.enter_context(tc.psum_pool(name="psum", bufs=8))
+        psum = stack.enter_context(tc.psum_pool(name="psum", bufs=PSUM_BANKS))
 
+        sources = {"anchor": anchor, "pos": pos}
         raw = {}
         for name in ("anchor", "pos"):
             raw[name] = keep.tile([P, ROW_TILES, FEATURES], BF16, name="raw_" + name)
-        for chunk in range(CHUNKS):
-            tiles = slice(chunk * CHUNK_TILES, (chunk + 1) * CHUNK_TILES)
-            for name, source in (("anchor", anchor), ("pos", pos)):
+        for name, chunk in CHUNK_ORDER:
+            for half in range(2):
+                first = chunk * CHUNK_TILES + half * HALF_TILES
                 nc.sync.dma_start(
-                    out=raw[name][:, tiles, :],
-                    in_=source.rearrange("(p r) k -> p r k", r=ROW_TILES)[:, tiles, :],
+                    out=raw[name][:, first : first + HALF_TILES, :],
+                    in_=sources[name].rearrange("(p r) k -> p r k", r=ROW_TILES)[
+                        :, first : first + HALF_TILES, :
+                    ],
                 )
 
         identity = keep.tile([P, P], F32)
@@ -54,6 +78,7 @@ def tile_crossgenderinfonceloss_pa_kernel(tc, anchor, pos, out):
         nc.vector.memset(zero[:], 0.0)
         one = keep.tile([P, 1], F32)
         nc.scalar.activation(out=one[:], in_=zero[:], func=ACT.Exp)
+        zero_again = keep.tile([P, 1], F32)
 
         mask_values = keep.tile([P, 2, P, PACK], BF16, align_bytes=64)
         spread_identity = identity[:].unsqueeze(2).to_broadcast([P, P, PACK])
@@ -80,32 +105,47 @@ def tile_crossgenderinfonceloss_pa_kernel(tc, anchor, pos, out):
         top = keep.tile([P, ROW_TILES * PARTS], F32)
         shift = keep.tile([P, ROW_TILES * PARTS], F32)
         total = keep.tile([P, ROW_TILES * PARTS], F32)
+        weight = keep.tile([P, 2, ROW_TILES, PARTS], F32)
+        nc.vector.memset(weight[:], FAR_BELOW)
 
-        def quantise_chunk(name, chunk):
+        grouped = {}
+
+        def flip_half(name, chunk, half):
+            if half == 0:
+                grouped[name, chunk] = stage_pool.tile(
+                    [P, BANK, PACK], BF16, name="grouped", align_bytes=64
+                )
             words = raw[name][:].bitcast(F32)
-            grouped = stage.tile([P, BANK, PACK], BF16, align_bytes=64)
-            grouped_words = grouped[:].bitcast(F32)
-            for pair in range(2):
-                flipped = psum.tile([P, 2, HALVES, P], F32, tag="bank")
-                for t in range(2):
-                    r = chunk * CHUNK_TILES + 2 * pair + t
-                    for u in range(HALVES):
-                        nc.tensor.transpose(
-                            flipped[:, t, u, :], words[:, r, u * P : (u + 1) * P], identity[:]
-                        )
-                target = grouped_words[:, 2 * pair * P : 2 * (pair + 1) * P, :]
-                target = target.rearrange("p (t r) u -> p t r u", t=2)
-                source = flipped[:].rearrange("p t u r -> p t r u")
-                if pair == 0:
-                    nc.vector.tensor_copy(out=target, in_=source)
-                else:
-                    nc.scalar.copy(out=target, in_=source)
+            flipped = psum.tile([P, HALF_TILES, WORD_HALVES, P], F32, tag="bank")
+            for t in range(HALF_TILES):
+                r = chunk * CHUNK_TILES + half * HALF_TILES + t
+                for u in range(WORD_HALVES):
+                    nc.tensor.transpose(
+                        flipped[:, t, u, :], words[:, r, u * P : (u + 1) * P], identity[:]
+                    )
+            rows = slice(half * HALF_TILES * P, (half + 1) * HALF_TILES * P)
+            target = grouped[name, chunk][:].bitcast(F32)[:, rows, :]
+            target = target.rearrange("p (t r) u -> p t r u", t=HALF_TILES)
+            source = flipped[:].rearrange("p t u r -> p t r u")
+            if name == "anchor":
+                nc.scalar.copy(out=target, in_=source)
+            else:
+                nc.vector.tensor_copy(out=target, in_=source)
+
+        def quantise(name, chunk):
             cols = slice(chunk * BANK, (chunk + 1) * BANK)
             nc.vector.quantize_mx(
                 out=codes[name][:, cols].bitcast(FP8X4),
                 scales=scales[name][:, cols],
-                in_=grouped[:].rearrange("p w j -> p (w j)"),
+                in_=grouped[name, chunk][:].rearrange("p w j -> p (w j)"),
             )
+
+        def steps_of(name, chunk):
+            return [
+                lambda: flip_half(name, chunk, 0),
+                lambda: flip_half(name, chunk, 1),
+                lambda: quantise(name, chunk),
+            ]
 
         def product(acc, r, name, cols, start, stop):
             rows = slice(r * P, (r + 1) * P)
@@ -119,7 +159,7 @@ def tile_crossgenderinfonceloss_pa_kernel(tc, anchor, pos, out):
                 stop=stop,
             )
 
-        def bank_of_logits(r, x, chunk):
+        def open_bank(r, x, chunk):
             acc = psum.tile([P, BANK], F32, tag="bank")
             if x == NEG and chunk == r // CHUNK_TILES:
                 for t in range(CHUNK_TILES):
@@ -149,6 +189,9 @@ def tile_crossgenderinfonceloss_pa_kernel(tc, anchor, pos, out):
                 op0=ALU.mult,
                 op1=ALU.add,
             )
+            return acc, col
+
+        def close_bank(acc, col):
             exps = unread.tile([P, BANK], BF16)
             nc.scalar.activation(
                 out=exps[:],
@@ -159,49 +202,60 @@ def tile_crossgenderinfonceloss_pa_kernel(tc, anchor, pos, out):
                 accum_out=total[:, col],
             )
 
-        for s in range(CHUNKS):
-            quantise_chunk("anchor", s)
-            quantise_chunk("pos", s)
-            for r in range((s + 1) * CHUNK_TILES):
-                for chunk in range(s + 1):
-                    if r // CHUNK_TILES == s or chunk == s:
-                        bank_of_logits(r, NEG, chunk)
-                        bank_of_logits(r, POS, chunk)
+        steps = []
+        for name, chunk in CHUNK_ORDER:
+            steps.extend(steps_of(name, chunk))
+        for step in steps[:HEAD_STEPS]:
+            step()
+        taken = HEAD_STEPS
+        still_open = None
+        for stage in range(len(CHUNK_ORDER)):
+            banks = banks_opened_by(stage)
+            due = min(len(steps), (stage + 2) * STEPS_PER_CHUNK)
+            every = (len(banks) - LEAD) // max(1, due - taken)
+            for n, (r, x, chunk) in enumerate(banks):
+                newest = open_bank(r, x, chunk)
+                if still_open is not None:
+                    close_bank(*still_open)
+                still_open = newest
+                if taken < due and (n + 1) % every == 0:
+                    steps[taken]()
+                    taken += 1
 
         shift_r = shift[:].rearrange("p (r b) -> p r b", b=PARTS)
         total_r = total[:].rearrange("p (r b) -> p r b", b=PARTS)
-        low_all = keep.tile([P, ROW_TILES], F32)
-        low_pos = keep.tile([P, ROW_TILES], F32)
-        nc.vector.tensor_reduce(out=low_all[:], in_=shift_r, axis=AXIS_X, op=ALU.min)
-        nc.vector.tensor_reduce(out=low_pos[:], in_=shift_r[:, :, 0:CHUNKS], axis=AXIS_X, op=ALU.min)
-        weight = keep.tile([P, ROW_TILES, PARTS + CHUNKS], F32)
+        low = keep.tile([P, 2, ROW_TILES], F32)
+        nc.vector.tensor_reduce(out=low[:, 0, :], in_=shift_r[:, :, 0:CHUNKS], axis=AXIS_X, op=ALU.min)
+        nc.vector.tensor_reduce(out=low[:, 1, :], in_=shift_r, axis=AXIS_X, op=ALU.min)
         nc.vector.tensor_tensor(
-            out=weight[:, :, 0:PARTS],
-            in0=low_all[:].unsqueeze(2).to_broadcast([P, ROW_TILES, PARTS]),
-            in1=shift_r,
-            op=ALU.subtract,
-        )
-        nc.vector.tensor_tensor(
-            out=weight[:, :, PARTS:],
-            in0=low_pos[:].unsqueeze(2).to_broadcast([P, ROW_TILES, CHUNKS]),
+            out=weight[:, 0, :, 0:CHUNKS],
+            in0=low[:, 0, :].unsqueeze(2).to_broadcast([P, ROW_TILES, CHUNKS]),
             in1=shift_r[:, :, 0:CHUNKS],
             op=ALU.subtract,
         )
-        nc.scalar.activation(out=weight[:], in_=weight[:], func=ACT.Exp)
         nc.vector.tensor_tensor(
-            out=weight[:, :, 0:PARTS], in0=weight[:, :, 0:PARTS], in1=total_r, op=ALU.mult
+            out=weight[:, 1],
+            in0=low[:, 1, :].unsqueeze(2).to_broadcast([P, ROW_TILES, PARTS]),
+            in1=shift_r,
+            op=ALU.subtract,
         )
+        gap = keep.tile([P, ROW_TILES], F32)
+        nc.vector.tensor_tensor(out=gap[:], in0=low[:, 1, :], in1=low[:, 0, :], op=ALU.subtract)
+        nc.scalar.activation(out=weight[:], in_=weight[:], func=ACT.Exp)
+        close_bank(*still_open)
+        nc.scalar.activation(out=zero_again[:], in_=one[:], func=ACT.Ln)
         nc.vector.tensor_tensor(
-            out=weight[:, :, PARTS:], in0=weight[:, :, PARTS:], in1=total_r[:, :, 0:CHUNKS], op=ALU.mult
+            out=weight[:],
+            in0=weight[:],
+            in1=total_r.unsqueeze(1).to_broadcast([P, 2, ROW_TILES, PARTS]),
+            op=ALU.mult,
         )
         sums = keep.tile([P, 2, ROW_TILES], F32)
-        nc.vector.tensor_reduce(out=sums[:, 0, :], in_=weight[:, :, PARTS:], axis=AXIS_X, op=ALU.add)
-        nc.vector.tensor_reduce(out=sums[:, 1, :], in_=weight[:, :, 0:PARTS], axis=AXIS_X, op=ALU.add)
-        logs = keep.tile([P, 2, ROW_TILES], F32)
-        nc.scalar.activation(out=logs[:], in_=sums[:], func=ACT.Ln)
-        gap = keep.tile([P, ROW_TILES], F32)
-        nc.vector.tensor_tensor(out=gap[:], in0=low_all[:], in1=low_pos[:], op=ALU.subtract)
+        nc.vector.tensor_reduce(out=sums[:], in_=weight[:], axis=AXIS_X, op=ALU.add)
+        ratio = keep.tile([P, ROW_TILES], F32)
+        nc.vector.reciprocal(out=ratio[:], in_=sums[:, 1, :])
+        nc.vector.tensor_tensor(out=ratio[:], in0=ratio[:], in1=sums[:, 0, :], op=ALU.mult)
         result = keep.tile([P, ROW_TILES], F32)
-        nc.vector.tensor_tensor(out=result[:], in0=logs[:, 0, :], in1=logs[:, 1, :], op=ALU.subtract)
+        nc.scalar.activation(out=result[:], in_=ratio[:], func=ACT.Ln)
         nc.vector.tensor_tensor(out=result[:], in0=result[:], in1=gap[:], op=ALU.add)
         nc.sync.dma_start(out=out.rearrange("(p r) -> p r", r=ROW_TILES), in_=result[:])

@@ -21,23 +21,24 @@ BANK = 512
 PSUM_BANKS = 8
 CHUNK_TILES = BANK // P
 CHUNKS = ROW_TILES // CHUNK_TILES
-HALF_TILES = CHUNK_TILES // 2
-WORD_HALVES = 2
+PAIR_TILES = 2
+PAIRS = CHUNK_TILES // PAIR_TILES
+SIDES = 2
 POS, NEG = 0, 1
-PARTS = 2 * CHUNKS
+PANELS = 2 * CHUNKS
 TEMPERATURE = 0.07
 MASK_ROOT = 2.0**50
 FAR_BELOW = -1.0e30
 
 CHUNK_ORDER = [("anchor", c) for c in range(CHUNKS)] + [("pos", c) for c in range(CHUNKS)]
-STEPS_PER_CHUNK = 3
-HEAD_STEPS = 2 * STEPS_PER_CHUNK + 2
+STEPS_PER_CHUNK = PAIRS + 1
+HEAD_STEPS = 2 * STEPS_PER_CHUNK + PAIRS
 LEAD = 2
 
 FLOPS = 2 * 2 * ROWS * ROWS * FEATURES
 
 
-def banks_opened_by(stage):
+def panels_opened_by(stage):
     name, chunk = CHUNK_ORDER[stage]
     if name == "pos":
         return [(r, POS, chunk) for r in range(ROW_TILES)]
@@ -54,7 +55,7 @@ def tile_crossgenderinfonceloss_pa_kernel(tc, anchor, pos, out):
     with ExitStack() as stack:
         stack.enter_context(tc.manual_schedule())
         keep = stack.enter_context(tc.tile_pool(name="keep", bufs=1))
-        stage_pool = stack.enter_context(tc.tile_pool(name="stage", bufs=3))
+        regroup = stack.enter_context(tc.tile_pool(name="regroup", bufs=3))
         unread = stack.enter_context(tc.tile_pool(name="unread", bufs=4))
         psum = stack.enter_context(tc.psum_pool(name="psum", bufs=PSUM_BANKS))
 
@@ -63,12 +64,12 @@ def tile_crossgenderinfonceloss_pa_kernel(tc, anchor, pos, out):
         for name in ("anchor", "pos"):
             raw[name] = keep.tile([P, ROW_TILES, FEATURES], BF16, name="raw_" + name)
         for name, chunk in CHUNK_ORDER:
-            for half in range(2):
-                first = chunk * CHUNK_TILES + half * HALF_TILES
+            for pair in range(PAIRS):
+                first = chunk * CHUNK_TILES + pair * PAIR_TILES
                 nc.sync.dma_start(
-                    out=raw[name][:, first : first + HALF_TILES, :],
+                    out=raw[name][:, first : first + PAIR_TILES, :],
                     in_=sources[name].rearrange("(p r) k -> p r k", r=ROW_TILES)[
-                        :, first : first + HALF_TILES, :
+                        :, first : first + PAIR_TILES, :
                     ],
                 )
 
@@ -78,7 +79,6 @@ def tile_crossgenderinfonceloss_pa_kernel(tc, anchor, pos, out):
         nc.vector.memset(zero[:], 0.0)
         one = keep.tile([P, 1], F32)
         nc.scalar.activation(out=one[:], in_=zero[:], func=ACT.Exp)
-        zero_again = keep.tile([P, 1], F32)
 
         mask_values = keep.tile([P, 2, P, PACK], BF16, align_bytes=64)
         spread_identity = identity[:].unsqueeze(2).to_broadcast([P, P, PACK])
@@ -102,31 +102,31 @@ def tile_crossgenderinfonceloss_pa_kernel(tc, anchor, pos, out):
             codes[name] = keep.tile([P, ROWS], U32, name="codes_" + name, align_bytes=64)
             scales[name] = keep.tile([P, ROWS], U8, name="scales_" + name, align_bytes=64)
 
-        top = keep.tile([P, ROW_TILES * PARTS], F32)
-        shift = keep.tile([P, ROW_TILES * PARTS], F32)
-        total = keep.tile([P, ROW_TILES * PARTS], F32)
-        weight = keep.tile([P, 2, ROW_TILES, PARTS], F32)
+        top = keep.tile([P, ROW_TILES * PANELS], F32)
+        shift = keep.tile([P, ROW_TILES * PANELS], F32)
+        total = keep.tile([P, ROW_TILES * PANELS], F32)
+        weight = keep.tile([P, 2, ROW_TILES, PANELS], F32)
         nc.vector.memset(weight[:], FAR_BELOW)
 
         grouped = {}
 
-        def flip_half(name, chunk, half):
-            if half == 0:
-                grouped[name, chunk] = stage_pool.tile(
+        def flip_pair(name, chunk, pair):
+            if pair == 0:
+                grouped[name, chunk] = regroup.tile(
                     [P, BANK, PACK], BF16, name="grouped", align_bytes=64
                 )
             words = raw[name][:].bitcast(F32)
-            flipped = psum.tile([P, HALF_TILES, WORD_HALVES, P], F32, tag="bank")
-            for t in range(HALF_TILES):
-                r = chunk * CHUNK_TILES + half * HALF_TILES + t
-                for u in range(WORD_HALVES):
+            flipped = psum.tile([P, PAIR_TILES, SIDES, P], F32, tag="bank")
+            for t in range(PAIR_TILES):
+                r = chunk * CHUNK_TILES + pair * PAIR_TILES + t
+                for side in range(SIDES):
                     nc.tensor.transpose(
-                        flipped[:, t, u, :], words[:, r, u * P : (u + 1) * P], identity[:]
+                        flipped[:, t, side, :], words[:, r, side * P : (side + 1) * P], identity[:]
                     )
-            rows = slice(half * HALF_TILES * P, (half + 1) * HALF_TILES * P)
+            rows = slice(pair * PAIR_TILES * P, (pair + 1) * PAIR_TILES * P)
             target = grouped[name, chunk][:].bitcast(F32)[:, rows, :]
-            target = target.rearrange("p (t r) u -> p t r u", t=HALF_TILES)
-            source = flipped[:].rearrange("p t u r -> p t r u")
+            target = target.rearrange("p (t m) side -> p t m side", t=PAIR_TILES)
+            source = flipped[:].rearrange("p t side m -> p t m side")
             if name == "anchor":
                 nc.scalar.copy(out=target, in_=source)
             else:
@@ -142,8 +142,8 @@ def tile_crossgenderinfonceloss_pa_kernel(tc, anchor, pos, out):
 
         def steps_of(name, chunk):
             return [
-                lambda: flip_half(name, chunk, 0),
-                lambda: flip_half(name, chunk, 1),
+                lambda: flip_pair(name, chunk, 0),
+                lambda: flip_pair(name, chunk, 1),
                 lambda: quantise(name, chunk),
             ]
 
@@ -159,7 +159,7 @@ def tile_crossgenderinfonceloss_pa_kernel(tc, anchor, pos, out):
                 stop=stop,
             )
 
-        def open_bank(r, x, chunk):
+        def open_panel(r, x, chunk):
             acc = psum.tile([P, BANK], F32, tag="bank")
             if x == NEG and chunk == r // CHUNK_TILES:
                 for t in range(CHUNK_TILES):
@@ -179,7 +179,7 @@ def tile_crossgenderinfonceloss_pa_kernel(tc, anchor, pos, out):
             else:
                 name = "pos" if x == POS else "anchor"
                 product(acc[:], r, name, slice(chunk * BANK, (chunk + 1) * BANK), True, True)
-            col = slice(r * PARTS + x * CHUNKS + chunk, r * PARTS + x * CHUNKS + chunk + 1)
+            col = slice(r * PANELS + x * CHUNKS + chunk, r * PANELS + x * CHUNKS + chunk + 1)
             nc.vector.tensor_reduce(out=top[:, col], in_=acc[:], axis=AXIS_X, op=ALU.max)
             nc.gpsimd.tensor_scalar(
                 out=shift[:, col],
@@ -191,7 +191,7 @@ def tile_crossgenderinfonceloss_pa_kernel(tc, anchor, pos, out):
             )
             return acc, col
 
-        def close_bank(acc, col):
+        def close_panel(acc, col):
             exps = unread.tile([P, BANK], BF16)
             nc.scalar.activation(
                 out=exps[:],
@@ -210,20 +210,20 @@ def tile_crossgenderinfonceloss_pa_kernel(tc, anchor, pos, out):
         taken = HEAD_STEPS
         still_open = None
         for stage in range(len(CHUNK_ORDER)):
-            banks = banks_opened_by(stage)
+            panels = panels_opened_by(stage)
             due = min(len(steps), (stage + 2) * STEPS_PER_CHUNK)
-            every = (len(banks) - LEAD) // max(1, due - taken)
-            for n, (r, x, chunk) in enumerate(banks):
-                newest = open_bank(r, x, chunk)
+            every = (len(panels) - LEAD) // max(1, due - taken)
+            for n, (r, x, chunk) in enumerate(panels):
+                newest = open_panel(r, x, chunk)
                 if still_open is not None:
-                    close_bank(*still_open)
+                    close_panel(*still_open)
                 still_open = newest
                 if taken < due and (n + 1) % every == 0:
                     steps[taken]()
                     taken += 1
 
-        shift_r = shift[:].rearrange("p (r b) -> p r b", b=PARTS)
-        total_r = total[:].rearrange("p (r b) -> p r b", b=PARTS)
+        shift_r = shift[:].rearrange("p (r b) -> p r b", b=PANELS)
+        total_r = total[:].rearrange("p (r b) -> p r b", b=PANELS)
         low = keep.tile([P, 2, ROW_TILES], F32)
         nc.vector.tensor_reduce(out=low[:, 0, :], in_=shift_r[:, :, 0:CHUNKS], axis=AXIS_X, op=ALU.min)
         nc.vector.tensor_reduce(out=low[:, 1, :], in_=shift_r, axis=AXIS_X, op=ALU.min)
@@ -235,19 +235,18 @@ def tile_crossgenderinfonceloss_pa_kernel(tc, anchor, pos, out):
         )
         nc.vector.tensor_tensor(
             out=weight[:, 1],
-            in0=low[:, 1, :].unsqueeze(2).to_broadcast([P, ROW_TILES, PARTS]),
+            in0=low[:, 1, :].unsqueeze(2).to_broadcast([P, ROW_TILES, PANELS]),
             in1=shift_r,
             op=ALU.subtract,
         )
         gap = keep.tile([P, ROW_TILES], F32)
         nc.vector.tensor_tensor(out=gap[:], in0=low[:, 1, :], in1=low[:, 0, :], op=ALU.subtract)
         nc.scalar.activation(out=weight[:], in_=weight[:], func=ACT.Exp)
-        close_bank(*still_open)
-        nc.scalar.activation(out=zero_again[:], in_=one[:], func=ACT.Ln)
+        close_panel(*still_open)
         nc.vector.tensor_tensor(
             out=weight[:],
             in0=weight[:],
-            in1=total_r.unsqueeze(1).to_broadcast([P, 2, ROW_TILES, PARTS]),
+            in1=total_r.unsqueeze(1).to_broadcast([P, 2, ROW_TILES, PANELS]),
             op=ALU.mult,
         )
         sums = keep.tile([P, 2, ROW_TILES], F32)

from contextlib import ExitStack

import concourse.mybir as mybir
from concourse.masks import make_identity

F32 = mybir.dt.float32
BF16 = mybir.dt.bfloat16
U32 = mybir.dt.uint32
U8 = mybir.dt.uint8
FP8X4 = mybir.dt.float8_e4m3fn_x4
ALU = mybir.AluOpType
ACT = mybir.ActivationFunctionType
AXIS_X = mybir.AxisListType.X

P = 128
PACK = 4
ROWS = 2048
FEATURES = 512
ROW_TILES = ROWS // P
BANK = 512
PSUM_BANKS = 8
CHUNK_TILES = BANK // P
CHUNKS = ROW_TILES // CHUNK_TILES
PAIR_TILES = 2
PAIRS = CHUNK_TILES // PAIR_TILES
SIDES = 2
POS, NEG = 0, 1
PANELS = 2 * CHUNKS
TEMPERATURE = 0.07
MASK_ROOT = 2.0**50
FAR_BELOW = -1.0e30

CHUNK_ORDER = [("anchor", c) for c in range(CHUNKS)] + [("pos", c) for c in range(CHUNKS)]
STEPS_PER_CHUNK = PAIRS + 1
HEAD_STEPS = 2 * STEPS_PER_CHUNK + PAIRS
LEAD = 2

FLOPS = 2 * 2 * ROWS * ROWS * FEATURES


def panels_opened_by(stage):
    name, chunk = CHUNK_ORDER[stage]
    if name == "pos":
        return [(r, POS, chunk) for r in range(ROW_TILES)]
    return [
        (r, NEG, c)
        for r in range((chunk + 1) * CHUNK_TILES)
        for c in range(chunk + 1)
        if r // CHUNK_TILES == chunk or c == chunk
    ]


def tile_crossgenderinfonceloss_pa_kernel(tc, anchor, pos, out):
    nc = tc.nc
    with ExitStack() as stack:
        stack.enter_context(tc.manual_schedule())
        keep = stack.enter_context(tc.tile_pool(name="keep", bufs=1))
        regroup = stack.enter_context(tc.tile_pool(name="regroup", bufs=3))
        unread = stack.enter_context(tc.tile_pool(name="unread", bufs=4))
        psum = stack.enter_context(tc.psum_pool(name="psum", bufs=PSUM_BANKS))

        sources = {"anchor": anchor, "pos": pos}
        raw = {}
        for name in ("anchor", "pos"):
            raw[name] = keep.tile([P, ROW_TILES, FEATURES], BF16, name="raw_" + name)
        for name, chunk in CHUNK_ORDER:
            for pair in range(PAIRS):
                first = chunk * CHUNK_TILES + pair * PAIR_TILES
                nc.sync.dma_start(
                    out=raw[name][:, first : first + PAIR_TILES, :],
                    in_=sources[name].rearrange("(p r) k -> p r k", r=ROW_TILES)[
                        :, first : first + PAIR_TILES, :
                    ],
                )

        identity = keep.tile([P, P], F32)
        make_identity(nc, identity[:])
        zero = keep.tile([P, 1], F32)
        nc.vector.memset(zero[:], 0.0)
        one = keep.tile([P, 1], F32)
        nc.scalar.activation(out=one[:], in_=zero[:], func=ACT.Exp)

        mask_values = keep.tile([P, 2, P, PACK], BF16, align_bytes=64)
        spread_identity = identity[:].unsqueeze(2).to_broadcast([P, P, PACK])
        nc.vector.tensor_scalar(
            out=mask_values[:, 0], in0=spread_identity, scalar1=MASK_ROOT, scalar2=None, op0=ALU.mult
        )
        nc.vector.tensor_scalar(
            out=mask_values[:, 1], in0=spread_identity, scalar1=-MASK_ROOT, scalar2=None, op0=ALU.mult
        )
        mask_codes = keep.tile([P, 2 * P], U32, align_bytes=64)
        mask_scales = keep.tile([P, 2 * P], U8, align_bytes=64)
        nc.vector.quantize_mx(
            out=mask_codes[:].bitcast(FP8X4),
            scales=mask_scales[:],
            in_=mask_values[:].rearrange("p s m j -> p (s m j)"),
        )

        codes = {}
        scales = {}
        for name in ("anchor", "pos"):
            codes[name] = keep.tile([P, ROWS], U32, name="codes_" + name, align_bytes=64)
            scales[name] = keep.tile([P, ROWS], U8, name="scales_" + name, align_bytes=64)

        top = keep.tile([P, ROW_TILES * PANELS], F32)
        shift = keep.tile([P, ROW_TILES * PANELS], F32)
        total = keep.tile([P, ROW_TILES * PANELS], F32)
        weight = keep.tile([P, 2, ROW_TILES, PANELS], F32)
        nc.vector.memset(weight[:], FAR_BELOW)

        grouped = {}

        def flip_pair(name, chunk, pair):
            if pair == 0:
                grouped[name, chunk] = regroup.tile(
                    [P, BANK, PACK], BF16, name="grouped", align_bytes=64
                )
            words = raw[name][:].bitcast(F32)
            flipped = psum.tile([P, PAIR_TILES, SIDES, P], F32, tag="bank")
            for t in range(PAIR_TILES):
                r = chunk * CHUNK_TILES + pair * PAIR_TILES + t
                for side in range(SIDES):
                    nc.tensor.transpose(
                        flipped[:, t, side, :], words[:, r, side * P : (side + 1) * P], identity[:]
                    )
            rows = slice(pair * PAIR_TILES * P, (pair + 1) * PAIR_TILES * P)
            target = grouped[name, chunk][:].bitcast(F32)[:, rows, :]
            target = target.rearrange("p (t m) side -> p t m side", t=PAIR_TILES)
            source = flipped[:].rearrange("p t side m -> p t m side")
            if name == "anchor":
                nc.scalar.copy(out=target, in_=source)
            else:
                nc.vector.tensor_copy(out=target, in_=source)

        def quantise(name, chunk):
            cols = slice(chunk * BANK, (chunk + 1) * BANK)
            nc.vector.quantize_mx(
                out=codes[name][:, cols].bitcast(FP8X4),
                scales=scales[name][:, cols],
                in_=grouped[name, chunk][:].rearrange("p w j -> p (w j)"),
            )

        def steps_of(name, chunk):
            return [
                lambda: flip_pair(name, chunk, 0),
                lambda: flip_pair(name, chunk, 1),
                lambda: quantise(name, chunk),
            ]

        def product(acc, r, name, cols, start, stop):
            rows = slice(r * P, (r + 1) * P)
            nc.tensor.matmul_mx(
                out=acc,
                lhsT=codes["anchor"][:, rows].bitcast(FP8X4),
                lhsT_scale=scales["anchor"][:, rows],
                rhs=codes[name][:, cols].bitcast(FP8X4),
                rhs_scale=scales[name][:, cols],
                start=start,
                stop=stop,
            )

        def open_panel(r, x, chunk):
            acc = psum.tile([P, BANK], F32, tag="bank")
            if x == NEG and chunk == r // CHUNK_TILES:
                for t in range(CHUNK_TILES):
                    other = chunk * CHUNK_TILES + t
                    part = acc[:, t * P : (t + 1) * P]
                    product(part, r, "anchor", slice(other * P, (other + 1) * P), True, other != r)
                    if other == r:
                        nc.tensor.matmul_mx(
                            out=part,
                            lhsT=mask_codes[:, 0:P].bitcast(FP8X4),
                            lhsT_scale=mask_scales[:, 0:P],
                            rhs=mask_codes[:, P : 2 * P].bitcast(FP8X4),
                            rhs_scale=mask_scales[:, P : 2 * P],
                            start=False,
                            stop=True,
                        )
            else:
                name = "pos" if x == POS else "anchor"
                product(acc[:], r, name, slice(chunk * BANK, (chunk + 1) * BANK), True, True)
            col = slice(r * PANELS + x * CHUNKS + chunk, r * PANELS + x * CHUNKS + chunk + 1)
            nc.vector.tensor_reduce(out=top[:, col], in_=acc[:], axis=AXIS_X, op=ALU.max)
            nc.gpsimd.tensor_scalar(
                out=shift[:, col],
                in0=top[:, col],
                scalar1=-1.0 / TEMPERATURE,
                scalar2=0.0,
                op0=ALU.mult,
                op1=ALU.add,
            )
            return acc, col

        def close_panel(acc, col):
            exps = unread.tile([P, BANK], BF16)
            nc.scalar.activation(
                out=exps[:],
                in_=acc[:],
                func=ACT.Exp,
                bias=shift[:, col],
                scale=1.0 / TEMPERATURE,
                accum_out=total[:, col],
            )

        steps = []
        for name, chunk in CHUNK_ORDER:
            steps.extend(steps_of(name, chunk))
        for step in steps[:HEAD_STEPS]:
            step()
        taken = HEAD_STEPS
        still_open = None
        for stage in range(len(CHUNK_ORDER)):
            panels = panels_opened_by(stage)
            due = min(len(steps), (stage + 2) * STEPS_PER_CHUNK)
            every = (len(panels) - LEAD) // max(1, due - taken)
            for n, (r, x, chunk) in enumerate(panels):
                newest = open_panel(r, x, chunk)
                if still_open is not None:
                    close_panel(*still_open)
                still_open = newest
                if taken < due and (n + 1) % every == 0:
                    steps[taken]()
                    taken += 1

        shift_r = shift[:].rearrange("p (r b) -> p r b", b=PANELS)
        total_r = total[:].rearrange("p (r b) -> p r b", b=PANELS)
        low = keep.tile([P, 2, ROW_TILES], F32)
        nc.vector.tensor_reduce(out=low[:, 0, :], in_=shift_r[:, :, 0:CHUNKS], axis=AXIS_X, op=ALU.min)
        nc.vector.tensor_reduce(out=low[:, 1, :], in_=shift_r, axis=AXIS_X, op=ALU.min)
        nc.vector.tensor_tensor(
            out=weight[:, 0, :, 0:CHUNKS],
            in0=low[:, 0, :].unsqueeze(2).to_broadcast([P, ROW_TILES, CHUNKS]),
            in1=shift_r[:, :, 0:CHUNKS],
            op=ALU.subtract,
        )
        nc.vector.tensor_tensor(
            out=weight[:, 1],
            in0=low[:, 1, :].unsqueeze(2).to_broadcast([P, ROW_TILES, PANELS]),
            in1=shift_r,
            op=ALU.subtract,
        )
        gap = keep.tile([P, ROW_TILES], F32)
        nc.vector.tensor_tensor(out=gap[:], in0=low[:, 1, :], in1=low[:, 0, :], op=ALU.subtract)
        nc.scalar.activation(out=weight[:], in_=weight[:], func=ACT.Exp)
        close_panel(*still_open)
        nc.vector.tensor_tensor(
            out=weight[:],
            in0=weight[:],
            in1=total_r.unsqueeze(1).to_broadcast([P, 2, ROW_TILES, PANELS]),
            op=ALU.mult,
        )
        sums = keep.tile([P, 2, ROW_TILES], F32)
        nc.vector.tensor_reduce(out=sums[:], in_=weight[:], axis=AXIS_X, op=ALU.add)
        ratio = keep.tile([P, ROW_TILES], F32)
        nc.vector.reciprocal(out=ratio[:], in_=sums[:, 1, :])
        nc.vector.tensor_tensor(out=ratio[:], in0=ratio[:], in1=sums[:, 0, :], op=ALU.mult)
        result = keep.tile([P, ROW_TILES], F32)
        nc.scalar.activation(out=result[:], in_=ratio[:], func=ACT.Ln)
        nc.vector.tensor_tensor(out=result[:], in0=result[:], in1=gap[:], op=ALU.add)
        nc.sync.dma_start(out=out.rearrange("(p r) -> p r", r=ROW_TILES), in_=result[:])
